import numpy as np
import ml_dtypes


def mxq(x, axis, fmt="e4m3"):
    dtype, down = {"e4m3": (ml_dtypes.float8_e4m3fn, 7), "e5m2": (ml_dtypes.float8_e5m2, 14)}[fmt]
    v = np.moveaxis(np.asarray(x, np.float32).astype(ml_dtypes.bfloat16).astype(np.float64), axis, -1)
    blocks = v.reshape(v.shape[:-1] + (-1, 32))
    amax = np.abs(blocks).max(-1, keepdims=True)
    byte = np.maximum(np.where(amax > 0, np.frexp(amax)[1] - 1 + 127, 0) - down, 1)
    scale = np.exp2(byte - 127.0)
    codes = (blocks / scale).astype(np.float32).astype(dtype).astype(np.float64)
    return np.moveaxis((codes * scale).reshape(v.shape), -1, axis)


WIDE = False


def mx_kscale(k):
    if not WIDE:
        return np.ones(k)
    levels = np.array([10, -10, 5, -5, 0])
    if k % 512:
        return np.exp2(np.random.permutation(np.resize(levels, k // 32))).repeat(32)
    a = np.empty((k // 512, 16))
    for p in range(k // 512):
        a[p, :8] = np.random.permutation(np.resize(levels, 8))
        for g in range(8):
            far = levels[np.abs(levels - a[p, g]) >= 10]
            a[p, g + 8] = far[np.random.randint(len(far))]
    return np.exp2(a.ravel()).repeat(32)


BF16 = ml_dtypes.bfloat16


def bf(x):
    return np.asarray(x, np.float32).astype(BF16)


def f64(x):
    return np.asarray(x).astype(np.float64)


B, IN, HID, PROJ, H, KC = 8192, 128, 512, 512, 4, 4
BH = HID // H
EPS = 1e-5


def silu(v):
    return v / (1.0 + np.exp(-v))


def groupnorm(v, w, b):
    r = v.reshape(B, H, BH)
    mu = r.mean(-1, keepdims=True)
    var = ((r - mu) ** 2).mean(-1, keepdims=True)
    rn = (r - mu) / np.sqrt(var + EPS)
    return rn.reshape(B, HID) * w + b


def setup_inputs():
    s, t = mx_kscale(PROJ), mx_kscale(HID)
    r = np.random.standard_normal
    return {"h_t": bf(r((B, HID)) * 0.5 / np.sqrt(HID)), "x_conv": bf(silu(r((B, PROJ))) * s),
            "x_right": bf(r((B, HID))), "x": bf(r((B, IN))),
            "gn_w": bf((1.0 + 0.1 * r(HID)) * t), "gn_b": bf(0.2 * r(HID) * t),
            "skip_w": bf(r((PROJ, HID)) * 1.5 / np.sqrt(PROJ) / s[:, None] * t[None, :]), "skip_b": bf(0.2 * r(HID) * t),
            "down_w": bf(r((HID, IN)) / np.sqrt(HID) / t[:, None]), "down_b": bf(0.2 * r(IN))}


def reference(h_t, x_conv, x_right, x, gn_w, gn_b, skip_w, skip_b, down_w, down_b):
    x_skip = (mxq(f64(x_conv), 1, "e4m3") @ mxq(f64(skip_w), 0, "e4m3")) + f64(skip_b)
    g = (groupnorm(f64(h_t), f64(gn_w), f64(gn_b)) + x_skip) * silu(f64(x_right))
    y = (mxq(g, 1, "e4m3") @ mxq(f64(down_w), 0, "e4m3")) + f64(down_b)
    return y + f64(x)

@@ -1,0 +1,321 @@
+from contextlib import ExitStack
+
+import concourse.mybir as mybir
+from concourse.masks import make_identity
+
+F32 = mybir.dt.float32
+BF16 = mybir.dt.bfloat16
+U32 = mybir.dt.uint32
+U8 = mybir.dt.uint8
+FP8X4 = mybir.dt.float8_e4m3fn_x4
+ALU = mybir.AluOpType
+ACT = mybir.ActivationFunctionType
+
+P = 128
+PACK = 4
+B, IN, HID, PROJ = 8192, 128, 512, 512
+GROUPS = 4
+GROUP = HID // GROUPS
+EPS = 1e-5
+TILES = 4
+BLOCK = TILES * P
+N_BLOCKS = B // BLOCK
+PAIR = 2
+LINE = 4
+
+FLOPS = 2 * B * PROJ * HID + 2 * B * HID * IN
+
+
+def quantise(nc, codes, scales, grouped):
+    nc.vector.quantize_mx(out=codes.bitcast(FP8X4), scales=scales, in_=grouped)
+
+
+def tile_mlstmblock_pc_t_kernel(
+    tc, h_t, x_conv, x_right, x, gn_w, gn_b, skip_w, skip_b, down_w, down_b, out
+):
+    nc = tc.nc
+    h_blocks = h_t.rearrange("(b p t) c -> b p t c", p=P, t=TILES)
+    xc_blocks = x_conv.rearrange("(b p t) c -> b p t c", p=P, t=TILES)
+    xr_blocks = x_right.rearrange("(b p t) c -> b p t c", p=P, t=TILES)
+    x_blocks = x.rearrange("(b p t) c -> b p t c", p=P, t=TILES)
+    out_blocks = out.rearrange("(b p t) c -> b p t c", p=P, t=TILES)
+
+    with ExitStack() as ctx:
+        consts = ctx.enter_context(tc.tile_pool(name="consts", bufs=1))
+        loads = ctx.enter_context(tc.tile_pool(name="loads", bufs=3))
+        work = ctx.enter_context(tc.tile_pool(name="work", bufs=2))
+        held = ctx.enter_context(tc.tile_pool(name="held", bufs=4))
+        small = ctx.enter_context(tc.tile_pool(name="small", bufs=4))
+        psum_in = ctx.enter_context(tc.psum_pool(name="psum_in", bufs=3))
+        psum_norm = ctx.enter_context(tc.psum_pool(name="psum_norm", bufs=2))
+        psum_skip = ctx.enter_context(tc.psum_pool(name="psum_skip", bufs=2))
+        psum_y = ctx.enter_context(tc.psum_pool(name="psum_y", bufs=1))
+
+        ident_f32 = consts.tile([P, P], F32)
+        make_identity(nc, ident_f32[:])
+        neg_half = consts.tile([P, TILES * GROUPS, 1], F32)
+        nc.vector.memset(neg_half[:], -0.5)
+
+        skip_raw = consts.tile([P, PACK, HID], BF16)
+        nc.scalar.dma_start(out=skip_raw[:], in_=skip_w.rearrange("(p k) c -> p k c", k=PACK))
+        down_raw = consts.tile([P, PACK, IN], BF16)
+        nc.scalar.dma_start(out=down_raw[:], in_=down_w.rearrange("(p k) c -> p k c", k=PACK))
+        vec_rows = consts.tile([P, HID], BF16)
+        nc.vector.memset(vec_rows[:], 0.0)
+        for v, vec in enumerate((gn_w, gn_b, skip_b)):
+            nc.gpsimd.dma_start(out=vec_rows[v : v + 1, :], in_=vec.unsqueeze(0))
+        down_b_all = consts.tile([P, IN], BF16)
+        nc.gpsimd.dma_start(out=down_b_all[:], in_=down_b.partition_broadcast(P))
+
+        skip_codes = consts.tile([P, HID], U32, align_bytes=64)
+        skip_scales = consts.tile([P, HID], U8, align_bytes=64)
+        down_codes = consts.tile([P, IN], U32, align_bytes=64)
+        down_scales = consts.tile([P, IN], U8, align_bytes=64)
+        vec_cols = consts.tile([P, 3 * PACK], F32)
+        gain = vec_cols[:, 0:PACK]
+        shift = consts.tile([P, PACK], F32)
+
+        def prepare_weights():
+            skip_grouped = consts.tile([P, PACK, P, PACK], BF16, align_bytes=64)
+            nc.vector.tensor_copy(out=skip_grouped[:], in_=skip_raw[:].rearrange("p k (m q) -> p q m k", q=PACK))
+            down_grouped = consts.tile([P, IN, PACK], BF16, align_bytes=64)
+            nc.vector.tensor_copy(out=down_grouped[:], in_=down_raw[:].rearrange("p k c -> p c k"))
+            quantise(nc, skip_codes[:], skip_scales[:], skip_grouped[:].rearrange("p q m k -> p (q m k)"))
+            quantise(nc, down_codes[:], down_scales[:], down_grouped[:].rearrange("p c k -> p (c k)"))
+            vec_t = psum_in.tile([P, PAIR, 2, P], F32, tag="in_t")
+            for u in range(2):
+                nc.tensor.transpose(vec_t[:, 0, u, :], vec_rows[:].bitcast(F32)[:, u::2], ident_f32[:])
+            nc.vector.tensor_copy(
+                out=vec_cols[:].rearrange("p (v u e) -> p v u e", v=3, u=2),
+                in_=vec_t[:, 0, :, :].bitcast(BF16)[:, :, 0:6].rearrange("p u (v e) -> p v u e", v=3),
+            )
+            nc.vector.tensor_tensor(
+                out=shift[:], in0=vec_cols[:, PACK : 2 * PACK], in1=vec_cols[:, 2 * PACK : 3 * PACK], op=ALU.add
+            )
+
+        tiles = {}
+
+        def load(b):
+            h_blk = loads.tile([P, TILES, HID], BF16)
+            nc.sync.dma_start(out=h_blk[:], in_=h_blocks[b])
+            xc_blk = loads.tile([P, TILES, PROJ], BF16)
+            nc.sync.dma_start(out=xc_blk[:], in_=xc_blocks[b])
+            xr_blk = loads.tile([P, TILES, HID], BF16)
+            nc.sync.dma_start(out=xr_blk[:], in_=xr_blocks[b])
+            x_blk = loads.tile([P, TILES, IN], BF16)
+            nc.sync.dma_start(out=x_blk[:], in_=x_blocks[b])
+            tiles["h", b], tiles["xc", b], tiles["xr", b], tiles["x", b] = h_blk, xc_blk, xr_blk, x_blk
+
+        def group_stats(b):
+            stats = small.tile([P, TILES * GROUPS, 3], F32)
+            for t in range(TILES):
+                for two in range(GROUPS // 2):
+                    nc.vector.bn_stats(
+                        out=stats[:, t * GROUPS + 2 * two : t * GROUPS + 2 * two + 2, :].rearrange("p g s -> p (g s)"),
+                        in_=tiles["h", b][:, t, 2 * two * GROUP : (2 * two + 2) * GROUP].rearrange(
+                            "p (g m) -> p m g", g=2
+                        ),
+                    )
+            tiles["stats", b] = stats
+
+        def rstd_and_residual(b):
+            mean, m2 = tiles["stats", b][:, :, 1:2], tiles["stats", b][:, :, 2:3]
+            neg_mean = small.tile([P, TILES * GROUPS, 1], F32)
+            nc.gpsimd.tensor_scalar(out=neg_mean[:], in0=mean, scalar1=-1.0, scalar2=0.0, op0=ALU.mult, op1=ALU.add)
+            var_eps = small.tile([P, TILES * GROUPS, 1], F32)
+            nc.gpsimd.tensor_scalar(out=var_eps[:], in0=m2, scalar1=1.0 / GROUP, scalar2=EPS, op0=ALU.mult, op1=ALU.add)
+            rstd = small.tile([P, TILES * GROUPS, 1], F32)
+            nc.gpsimd.tensor_tensor(out=rstd[:], in0=var_eps[:], in1=neg_half[:], op=ALU.pow)
+            neg_mean_rstd = small.tile([P, TILES * GROUPS, 1], F32)
+            nc.gpsimd.tensor_tensor(out=neg_mean_rstd[:], in0=neg_mean[:], in1=rstd[:], op=ALU.mult)
+            tiles["rstd", b], tiles["neg_mean_rstd", b] = rstd, neg_mean_rstd
+            residual = held.tile([P, TILES, IN], F32, bufs=5)
+            nc.gpsimd.tensor_tensor(
+                out=residual[:],
+                in0=tiles["x", b][:],
+                in1=down_b_all[:].unsqueeze(1).to_broadcast([P, TILES, IN]),
+                op=ALU.add,
+            )
+            tiles["residual", b] = residual
+
+        def normalise(b, t):
+            if t == 0:
+                norm = work.tile([P, TILES, PACK, P], F32)
+                tiles["norm", b] = norm
+            for j in range(GROUPS):
+                m0 = j * (P // GROUPS)
+                nc.scalar.activation(
+                    out=tiles["norm", b][:, t, :, m0 : m0 + P // GROUPS],
+                    in_=tiles["h", b][:, t, j * GROUP : (j + 1) * GROUP].rearrange("p (m q) -> p q m", q=PACK),
+                    func=ACT.Identity,
+                    scale=tiles["rstd", b][:, t * GROUPS + j, :],
+                    bias=tiles["neg_mean_rstd", b][:, t * GROUPS + j, :],
+                )
+
+        def transpose_words(b, name, pair):
+            words = tiles[name, b][:].bitcast(F32)
+            in_t = psum_in.tile([P, PAIR, 2, P], F32)
+            for i in range(PAIR):
+                for u in range(2):
+                    nc.tensor.transpose(in_t[:, i, u, :], words[:, pair * PAIR + i, u::2], ident_f32[:])
+            tiles[name + "_t", b, pair] = in_t
+
+        def group_x_conv(b, pair):
+            if pair == 0:
+                xc_grouped = work.tile([P, TILES, P, PACK], BF16, align_bytes=64)
+                tiles["xc_grouped", b] = xc_grouped
+            nc.scalar.copy(
+                out=tiles["xc_grouped", b][:].bitcast(F32)[:, pair * PAIR : (pair + 1) * PAIR, :, :],
+                in_=tiles["xc_t", b, pair][:].rearrange("p i u r -> p i r u"),
+            )
+
+        def quantise_x_conv(b):
+            xc_codes = held.tile([P, TILES * P], U32, align_bytes=64)
+            xc_scales = held.tile([P, TILES * P], U8, align_bytes=64)
+            quantise(nc, xc_codes[:], xc_scales[:], tiles["xc_grouped", b][:].rearrange("p t r q -> p (t r q)"))
+            tiles["xc_codes", b], tiles["xc_scales", b] = xc_codes, xc_scales
+
+        def silu_gate(b, t):
+            if t == 0:
+                gate = held.tile([P, TILES, P, PACK], F32)
+                tiles["gate", b] = gate
+            nc.scalar.activation(
+                out=tiles["gate", b][:, t, :, :].rearrange("p r (u e) -> p r u e", e=2),
+                in_=tiles["xr_t", b, t // PAIR][:, t % PAIR, :, :].bitcast(BF16).rearrange("p u (r e) -> p r u e", e=2),
+                func=ACT.Silu,
+            )
+
+        def transpose_norm(b, q):
+            norm_t = psum_norm.tile([P, TILES, P], F32)
+            for t in range(TILES):
+                nc.tensor.transpose(norm_t[:, t, :], tiles["norm", b][:, t, q, :], ident_f32[:])
+            tiles["norm_t", b, q] = norm_t
+
+        def gain_and_biases(b, q):
+            if q == 0:
+                gn = work.tile([P, PACK, TILES, P], F32)
+                tiles["gn", b] = gn
+            nc.scalar.activation(
+                out=tiles["gn", b][:, q, :, :],
+                in_=tiles["norm_t", b, q][:],
+                func=ACT.Identity,
+                scale=gain[:, q : q + 1],
+                bias=shift[:, q : q + 1],
+            )
+
+        def skip_product(b, t):
+            rows = slice(t * P, (t + 1) * P)
+            skip_t = psum_skip.tile([P, PACK, P], F32)
+            for q in range(PACK):
+                cols = slice(q * P, (q + 1) * P)
+                nc.tensor.matmul_mx(
+                    out=skip_t[:, q, :],
+                    lhsT=skip_codes[:, cols].bitcast(FP8X4),
+                    lhsT_scale=skip_scales[:, cols],
+                    rhs=tiles["xc_codes", b][:, rows].bitcast(FP8X4),
+                    rhs_scale=tiles["xc_scales", b][:, rows],
+                    start=True,
+                    stop=True,
+                )
+            tiles["skip_t", b, t] = skip_t
+
+        def add_streams(b, t):
+            summed = work.tile([P, P, PACK], F32, bufs=4)
+            nc.vector.tensor_tensor(
+                out=summed[:].rearrange("p (c i) q -> p c q i", i=LINE),
+                in0=tiles["skip_t", b, t][:].rearrange("p q (c i) -> p c q i", i=LINE),
+                in1=tiles["gn", b][:, :, t, :].rearrange("p q (c i) -> p c q i", i=LINE),
+                op=ALU.add,
+            )
+            tiles["summed", b, t] = summed
+
+        def apply_gate(b, t):
+            if t == 0:
+                g_grouped = work.tile([P, TILES, P, PACK], BF16, align_bytes=64)
+                tiles["g_grouped", b] = g_grouped
+            nc.vector.tensor_tensor(
+                out=tiles["g_grouped", b][:, t, :, :],
+                in0=tiles["summed", b, t][:],
+                in1=tiles["gate", b][:, t, :, :],
+                op=ALU.mult,
+            )
+
+        def quantise_g(b):
+            g_codes = work.tile([P, TILES * P], U32, align_bytes=64)
+            g_scales = work.tile([P, TILES * P], U8, align_bytes=64)
+            quantise(nc, g_codes[:], g_scales[:], tiles["g_grouped", b][:].rearrange("p t r q -> p (t r q)"))
+            tiles["g_codes", b], tiles["g_scales", b] = g_codes, g_scales
+
+        def down_product(b):
+            y = psum_y.tile([P, TILES, IN], F32)
+            for t in range(TILES):
+                rows = slice(t * P, (t + 1) * P)
+                nc.tensor.matmul_mx(
+                    out=y[:, t, :],
+                    lhsT=tiles["g_codes", b][:, rows].bitcast(FP8X4),
+                    lhsT_scale=tiles["g_scales", b][:, rows],
+                    rhs=down_codes[:].bitcast(FP8X4),
+                    rhs_scale=down_scales[:],
+                    start=True,
+                    stop=True,
+                )
+            tiles["y", b] = y
+
+        def add_residual_and_store(b):
+            result = work.tile([P, TILES, IN], F32)
+            nc.vector.tensor_tensor(out=result[:], in0=tiles["y", b][:], in1=tiles["residual", b][:], op=ALU.add)
+            nc.sync.dma_start(out=out_blocks[b], in_=result[:])
+
+        def run(piece, b, *part):
+            if 0 <= b < N_BLOCKS:
+                piece(b, *part)
+
+        def turn(i):
+            run(load, i + 3)
+            run(skip_product, i - 1, 0)
+            run(skip_product, i - 1, 1)
+            run(transpose_words, i + 2, "xc", 0)
+            run(transpose_words, i + 2, "xc", 1)
+            run(transpose_norm, i, 0)
+            run(transpose_norm, i, 1)
+            run(group_x_conv, i + 2, 0)
+            run(group_x_conv, i + 2, 1)
+            run(gain_and_biases, i, 0)
+            run(gain_and_biases, i, 1)
+            run(normalise, i + 1, 0)
+            run(normalise, i + 1, 1)
+            run(add_streams, i - 1, 0)
+            run(add_streams, i - 1, 1)
+            run(group_stats, i + 2)
+            run(rstd_and_residual, i + 2)
+            run(down_product, i - 2)
+            run(skip_product, i - 1, 2)
+            run(skip_product, i - 1, 3)
+            run(transpose_words, i + 2, "xr", 0)
+            run(transpose_words, i + 2, "xr", 1)
+            run(transpose_norm, i, 2)
+            run(transpose_norm, i, 3)
+            run(silu_gate, i + 2, 0)
+            run(silu_gate, i + 2, 1)
+            run(gain_and_biases, i, 2)
+            run(silu_gate, i + 2, 2)
+            run(silu_gate, i + 2, 3)
+            run(gain_and_biases, i, 3)
+            run(normalise, i + 1, 2)
+            run(normalise, i + 1, 3)
+            run(add_streams, i - 1, 2)
+            run(add_streams, i - 1, 3)
+            run(apply_gate, i - 1, 0)
+            run(apply_gate, i - 1, 1)
+            run(quantise_x_conv, i + 2)
+            run(apply_gate, i - 1, 2)
+            run(apply_gate, i - 1, 3)
+            run(add_residual_and_store, i - 2)
+            run(quantise_g, i - 1)
+
+        with tc.manual_schedule():
+            turn(-3)
+            turn(-2)
+            prepare_weights()
+            for i in range(-1, N_BLOCKS + 2):
+                turn(i)

@@ -42,10 +42,10 @@ def tile_mlstmblock_pc_t_kernel(
 
     with ExitStack() as ctx:
         consts = ctx.enter_context(tc.tile_pool(name="consts", bufs=1))
-        loads = ctx.enter_context(tc.tile_pool(name="loads", bufs=3))
+        loads = ctx.enter_context(tc.tile_pool(name="loads", bufs=4))
         work = ctx.enter_context(tc.tile_pool(name="work", bufs=2))
         held = ctx.enter_context(tc.tile_pool(name="held", bufs=4))
-        small = ctx.enter_context(tc.tile_pool(name="small", bufs=4))
+        small = ctx.enter_context(tc.tile_pool(name="small", bufs=6))
         psum_in = ctx.enter_context(tc.psum_pool(name="psum_in", bufs=3))
         psum_norm = ctx.enter_context(tc.psum_pool(name="psum_norm", bufs=2))
         psum_skip = ctx.enter_context(tc.psum_pool(name="psum_skip", bufs=2))
@@ -56,14 +56,14 @@ def tile_mlstmblock_pc_t_kernel(
         neg_half = consts.tile([P, TILES * GROUPS, 1], F32)
         nc.vector.memset(neg_half[:], -0.5)
 
+        vec_rows = consts.tile([P, HID], BF16)
+        nc.vector.memset(vec_rows[:], 0.0)
+        for v, vec in enumerate((gn_w, gn_b, skip_b)):
+            nc.scalar.dma_start(out=vec_rows[v : v + 1, :], in_=vec.unsqueeze(0))
         skip_raw = consts.tile([P, PACK, HID], BF16)
         nc.scalar.dma_start(out=skip_raw[:], in_=skip_w.rearrange("(p k) c -> p k c", k=PACK))
         down_raw = consts.tile([P, PACK, IN], BF16)
         nc.scalar.dma_start(out=down_raw[:], in_=down_w.rearrange("(p k) c -> p k c", k=PACK))
-        vec_rows = consts.tile([P, HID], BF16)
-        nc.vector.memset(vec_rows[:], 0.0)
-        for v, vec in enumerate((gn_w, gn_b, skip_b)):
-            nc.gpsimd.dma_start(out=vec_rows[v : v + 1, :], in_=vec.unsqueeze(0))
         down_b_all = consts.tile([P, IN], BF16)
         nc.gpsimd.dma_start(out=down_b_all[:], in_=down_b.partition_broadcast(P))
 
@@ -82,12 +82,14 @@ def tile_mlstmblock_pc_t_kernel(
             nc.vector.tensor_copy(out=down_grouped[:], in_=down_raw[:].rearrange("p k c -> p c k"))
             quantise(nc, skip_codes[:], skip_scales[:], skip_grouped[:].rearrange("p q m k -> p (q m k)"))
             quantise(nc, down_codes[:], down_scales[:], down_grouped[:].rearrange("p c k -> p (c k)"))
-            vec_t = psum_in.tile([P, PAIR, 2, P], F32, tag="in_t")
+
+        def prepare_vectors():
+            vec_t = psum_in.tile([P, 2, PAIR, P], F32, tag="in_t")
             for u in range(2):
-                nc.tensor.transpose(vec_t[:, 0, u, :], vec_rows[:].bitcast(F32)[:, u::2], ident_f32[:])
+                nc.tensor.transpose(vec_t[:, u, 0, :], vec_rows[:].bitcast(F32)[:, u::2], ident_f32[:])
             nc.vector.tensor_copy(
                 out=vec_cols[:].rearrange("p (v u e) -> p v u e", v=3, u=2),
-                in_=vec_t[:, 0, :, :].bitcast(BF16)[:, :, 0:6].rearrange("p u (v e) -> p v u e", v=3),
+                in_=vec_t[:, :, 0, :].bitcast(BF16)[:, :, 0:6].rearrange("p u (v e) -> p v u e", v=3),
             )
             nc.vector.tensor_tensor(
                 out=shift[:], in0=vec_cols[:, PACK : 2 * PACK], in1=vec_cols[:, 2 * PACK : 3 * PACK], op=ALU.add
@@ -95,16 +97,19 @@ def tile_mlstmblock_pc_t_kernel(
 
         tiles = {}
 
-        def load(b):
-            h_blk = loads.tile([P, TILES, HID], BF16)
+        def load_h(b):
+            h_blk = loads.tile([P, TILES, HID], BF16, bufs=7)
             nc.sync.dma_start(out=h_blk[:], in_=h_blocks[b])
+            tiles["h", b] = h_blk
+
+        def load_rest(b):
             xc_blk = loads.tile([P, TILES, PROJ], BF16)
             nc.sync.dma_start(out=xc_blk[:], in_=xc_blocks[b])
             xr_blk = loads.tile([P, TILES, HID], BF16)
             nc.sync.dma_start(out=xr_blk[:], in_=xr_blocks[b])
             x_blk = loads.tile([P, TILES, IN], BF16)
             nc.sync.dma_start(out=x_blk[:], in_=x_blocks[b])
-            tiles["h", b], tiles["xc", b], tiles["xr", b], tiles["x", b] = h_blk, xc_blk, xr_blk, x_blk
+            tiles["xc", b], tiles["xr", b], tiles["x", b] = xc_blk, xr_blk, x_blk
 
         def group_stats(b):
             stats = small.tile([P, TILES * GROUPS, 3], F32)
@@ -118,7 +123,7 @@ def tile_mlstmblock_pc_t_kernel(
                     )
             tiles["stats", b] = stats
 
-        def rstd_and_residual(b):
+        def rstd_of_groups(b):
             mean, m2 = tiles["stats", b][:, :, 1:2], tiles["stats", b][:, :, 2:3]
             neg_mean = small.tile([P, TILES * GROUPS, 1], F32)
             nc.gpsimd.tensor_scalar(out=neg_mean[:], in0=mean, scalar1=-1.0, scalar2=0.0, op0=ALU.mult, op1=ALU.add)
@@ -129,6 +134,8 @@ def tile_mlstmblock_pc_t_kernel(
             neg_mean_rstd = small.tile([P, TILES * GROUPS, 1], F32)
             nc.gpsimd.tensor_tensor(out=neg_mean_rstd[:], in0=neg_mean[:], in1=rstd[:], op=ALU.mult)
             tiles["rstd", b], tiles["neg_mean_rstd", b] = rstd, neg_mean_rstd
+
+        def add_bias(b):
             residual = held.tile([P, TILES, IN], F32, bufs=5)
             nc.gpsimd.tensor_tensor(
                 out=residual[:],
@@ -154,10 +161,10 @@ def tile_mlstmblock_pc_t_kernel(
 
         def transpose_words(b, name, pair):
             words = tiles[name, b][:].bitcast(F32)
-            in_t = psum_in.tile([P, PAIR, 2, P], F32)
+            in_t = psum_in.tile([P, 2, PAIR, P], F32)
             for i in range(PAIR):
                 for u in range(2):
-                    nc.tensor.transpose(in_t[:, i, u, :], words[:, pair * PAIR + i, u::2], ident_f32[:])
+                    nc.tensor.transpose(in_t[:, u, i, :], words[:, pair * PAIR + i, u::2], ident_f32[:])
             tiles[name + "_t", b, pair] = in_t
 
         def group_x_conv(b, pair):
@@ -166,7 +173,7 @@ def tile_mlstmblock_pc_t_kernel(
                 tiles["xc_grouped", b] = xc_grouped
             nc.scalar.copy(
                 out=tiles["xc_grouped", b][:].bitcast(F32)[:, pair * PAIR : (pair + 1) * PAIR, :, :],
-                in_=tiles["xc_t", b, pair][:].rearrange("p i u r -> p i r u"),
+                in_=tiles["xc_t", b, pair][:].rearrange("p u i r -> p i r u"),
             )
 
         def quantise_x_conv(b):
@@ -175,13 +182,14 @@ def tile_mlstmblock_pc_t_kernel(
             quantise(nc, xc_codes[:], xc_scales[:], tiles["xc_grouped", b][:].rearrange("p t r q -> p (t r q)"))
             tiles["xc_codes", b], tiles["xc_scales", b] = xc_codes, xc_scales
 
-        def silu_gate(b, t):
-            if t == 0:
-                gate = held.tile([P, TILES, P, PACK], F32)
+        def silu_gate(b, pair):
+            if pair == 0:
+                gate = held.tile([P, BLOCK, PACK], F32)
                 tiles["gate", b] = gate
+            rows = slice(pair * PAIR * P, (pair + 1) * PAIR * P)
             nc.scalar.activation(
-                out=tiles["gate", b][:, t, :, :].rearrange("p r (u e) -> p r u e", e=2),
-                in_=tiles["xr_t", b, t // PAIR][:, t % PAIR, :, :].bitcast(BF16).rearrange("p u (r e) -> p r u e", e=2),
+                out=tiles["gate", b][:, rows, :].rearrange("p r (u e) -> p r u e", e=2),
+                in_=tiles["xr_t", b, pair][:].rearrange("p u i r -> p u (i r)").bitcast(BF16).rearrange("p u (r e) -> p r u e", e=2),
                 func=ACT.Silu,
             )
 
@@ -220,30 +228,32 @@ def tile_mlstmblock_pc_t_kernel(
             tiles["skip_t", b, t] = skip_t
 
         def add_streams(b, t):
-            summed = work.tile([P, P, PACK], F32, bufs=4)
+            if t == 0:
+                summed = work.tile([P, BLOCK, PACK], F32)
+                tiles["summed", b] = summed
             nc.vector.tensor_tensor(
-                out=summed[:].rearrange("p (c i) q -> p c q i", i=LINE),
+                out=tiles["summed", b][:, t * P : (t + 1) * P, :].rearrange("p (c i) q -> p c q i", i=LINE),
                 in0=tiles["skip_t", b, t][:].rearrange("p q (c i) -> p c q i", i=LINE),
                 in1=tiles["gn", b][:, :, t, :].rearrange("p q (c i) -> p c q i", i=LINE),
                 op=ALU.add,
             )
-            tiles["summed", b, t] = summed
 
-        def apply_gate(b, t):
-            if t == 0:
-                g_grouped = work.tile([P, TILES, P, PACK], BF16, align_bytes=64)
+        def apply_gate(b, pair):
+            if pair == 0:
+                g_grouped = work.tile([P, BLOCK, PACK], BF16, align_bytes=64)
                 tiles["g_grouped", b] = g_grouped
+            rows = slice(pair * PAIR * P, (pair + 1) * PAIR * P)
             nc.vector.tensor_tensor(
-                out=tiles["g_grouped", b][:, t, :, :],
-                in0=tiles["summed", b, t][:],
-                in1=tiles["gate", b][:, t, :, :],
+                out=tiles["g_grouped", b][:, rows, :],
+                in0=tiles["summed", b][:, rows, :],
+                in1=tiles["gate", b][:, rows, :],
                 op=ALU.mult,
             )
 
         def quantise_g(b):
             g_codes = work.tile([P, TILES * P], U32, align_bytes=64)
             g_scales = work.tile([P, TILES * P], U8, align_bytes=64)
-            quantise(nc, g_codes[:], g_scales[:], tiles["g_grouped", b][:].rearrange("p t r q -> p (t r q)"))
+            quantise(nc, g_codes[:], g_scales[:], tiles["g_grouped", b][:].rearrange("p r q -> p (r q)"))
             tiles["g_codes", b], tiles["g_scales", b] = g_codes, g_scales
 
         def down_product(b):
@@ -271,7 +281,10 @@ def tile_mlstmblock_pc_t_kernel(
                 piece(b, *part)
 
         def turn(i):
-            run(load, i + 3)
+            if i + 6 > 0:
+                run(load_h, i + 6)
+            if i + 4 > 0:
+                run(load_rest, i + 4)
             run(skip_product, i - 1, 0)
             run(skip_product, i - 1, 1)
             run(transpose_words, i + 2, "xc", 0)
@@ -286,8 +299,9 @@ def tile_mlstmblock_pc_t_kernel(
             run(normalise, i + 1, 1)
             run(add_streams, i - 1, 0)
             run(add_streams, i - 1, 1)
-            run(group_stats, i + 2)
-            run(rstd_and_residual, i + 2)
+            run(group_stats, i + 5)
+            run(rstd_of_groups, i + 5)
+            run(add_bias, i + 2)
             run(down_product, i - 2)
             run(skip_product, i - 1, 2)
             run(skip_product, i - 1, 3)
@@ -296,26 +310,26 @@ def tile_mlstmblock_pc_t_kernel(
             run(transpose_norm, i, 2)
             run(transpose_norm, i, 3)
             run(silu_gate, i + 2, 0)
-            run(silu_gate, i + 2, 1)
             run(gain_and_biases, i, 2)
-            run(silu_gate, i + 2, 2)
-            run(silu_gate, i + 2, 3)
+            run(silu_gate, i + 2, 1)
             run(gain_and_biases, i, 3)
             run(normalise, i + 1, 2)
             run(normalise, i + 1, 3)
             run(add_streams, i - 1, 2)
             run(add_streams, i - 1, 3)
             run(apply_gate, i - 1, 0)
-            run(apply_gate, i - 1, 1)
             run(quantise_x_conv, i + 2)
-            run(apply_gate, i - 1, 2)
-            run(apply_gate, i - 1, 3)
+            run(apply_gate, i - 1, 1)
             run(add_residual_and_store, i - 2)
             run(quantise_g, i - 1)
 
         with tc.manual_schedule():
-            turn(-3)
-            turn(-2)
+            load_h(0)
+            load_rest(0)
+            for i in range(-5, -1):
+                turn(i)
             prepare_weights()
-            for i in range(-1, N_BLOCKS + 2):
+            turn(-1)
+            prepare_vectors()
+            for i in range(N_BLOCKS + 2):
                 turn(i)

@@ -21,6 +21,7 @@ TILES = 4
 BLOCK = TILES * P
 N_BLOCKS = B // BLOCK
 PAIR = 2
+NORM_ON_GPSIMD = (3,)
 LINE = 4
 
 FLOPS = 2 * B * PROJ * HID + 2 * B * HID * IN
@@ -46,9 +47,9 @@ def tile_mlstmblock_pc_t_kernel(
         work = ctx.enter_context(tc.tile_pool(name="work", bufs=2))
         held = ctx.enter_context(tc.tile_pool(name="held", bufs=4))
         small = ctx.enter_context(tc.tile_pool(name="small", bufs=6))
-        psum_in = ctx.enter_context(tc.psum_pool(name="psum_in", bufs=3))
+        psum_in = ctx.enter_context(tc.psum_pool(name="psum_in", bufs=2))
         psum_norm = ctx.enter_context(tc.psum_pool(name="psum_norm", bufs=2))
-        psum_skip = ctx.enter_context(tc.psum_pool(name="psum_skip", bufs=2))
+        psum_skip = ctx.enter_context(tc.psum_pool(name="psum_skip", bufs=3))
         psum_y = ctx.enter_context(tc.psum_pool(name="psum_y", bufs=1))
 
         ident_f32 = consts.tile([P, P], F32)
@@ -84,12 +85,12 @@ def tile_mlstmblock_pc_t_kernel(
             quantise(nc, down_codes[:], down_scales[:], down_grouped[:].rearrange("p c k -> p (c k)"))
 
         def prepare_vectors():
-            vec_t = psum_in.tile([P, 2, PAIR, P], F32, tag="in_t")
+            vec_t = psum_y.tile([P, TILES, IN], F32, tag="y")
             for u in range(2):
-                nc.tensor.transpose(vec_t[:, u, 0, :], vec_rows[:].bitcast(F32)[:, u::2], ident_f32[:])
+                nc.tensor.transpose(vec_t[:, u, :], vec_rows[:].bitcast(F32)[:, u::2], ident_f32[:])
             nc.vector.tensor_copy(
                 out=vec_cols[:].rearrange("p (v u e) -> p v u e", v=3, u=2),
-                in_=vec_t[:, :, 0, :].bitcast(BF16)[:, :, 0:6].rearrange("p u (v e) -> p v u e", v=3),
+                in_=vec_t[:, 0:2, :].bitcast(BF16)[:, :, 0:6].rearrange("p u (v e) -> p v u e", v=3),
             )
             nc.vector.tensor_tensor(
                 out=shift[:], in0=vec_cols[:, PACK : 2 * PACK], in1=vec_cols[:, 2 * PACK : 3 * PACK], op=ALU.add
@@ -98,7 +99,7 @@ def tile_mlstmblock_pc_t_kernel(
         tiles = {}
 
         def load_h(b):
-            h_blk = loads.tile([P, TILES, HID], BF16, bufs=7)
+            h_blk = loads.tile([P, TILES, HID], BF16, bufs=4)
             nc.sync.dma_start(out=h_blk[:], in_=h_blocks[b])
             tiles["h", b] = h_blk
 
@@ -146,18 +147,21 @@ def tile_mlstmblock_pc_t_kernel(
             tiles["residual", b] = residual
 
         def normalise(b, t):
-            if t == 0:
+            if ("norm", b) not in tiles:
                 norm = work.tile([P, TILES, PACK, P], F32)
                 tiles["norm", b] = norm
             for j in range(GROUPS):
                 m0 = j * (P // GROUPS)
-                nc.scalar.activation(
-                    out=tiles["norm", b][:, t, :, m0 : m0 + P // GROUPS],
-                    in_=tiles["h", b][:, t, j * GROUP : (j + 1) * GROUP].rearrange("p (m q) -> p q m", q=PACK),
-                    func=ACT.Identity,
-                    scale=tiles["rstd", b][:, t * GROUPS + j, :],
-                    bias=tiles["neg_mean_rstd", b][:, t * GROUPS + j, :],
-                )
+                normed = tiles["norm", b][:, t, :, m0 : m0 + P // GROUPS]
+                raw = tiles["h", b][:, t, j * GROUP : (j + 1) * GROUP].rearrange("p (m q) -> p q m", q=PACK)
+                rstd = tiles["rstd", b][:, t * GROUPS + j, :]
+                neg_mean_rstd = tiles["neg_mean_rstd", b][:, t * GROUPS + j, :]
+                if t in NORM_ON_GPSIMD:
+                    nc.gpsimd.tensor_scalar(
+                        out=normed, in0=raw, scalar1=rstd, scalar2=neg_mean_rstd, op0=ALU.mult, op1=ALU.add
+                    )
+                else:
+                    nc.scalar.activation(out=normed, in_=raw, func=ACT.Identity, scale=rstd, bias=neg_mean_rstd)
 
         def transpose_words(b, name, pair):
             words = tiles[name, b][:].bitcast(F32)
@@ -281,55 +285,52 @@ def tile_mlstmblock_pc_t_kernel(
                 piece(b, *part)
 
         def turn(i):
-            if i + 6 > 0:
-                run(load_h, i + 6)
-            if i + 4 > 0:
-                run(load_rest, i + 4)
-            run(skip_product, i - 1, 0)
-            run(skip_product, i - 1, 1)
-            run(transpose_words, i + 2, "xc", 0)
-            run(transpose_words, i + 2, "xc", 1)
-            run(transpose_norm, i, 0)
-            run(transpose_norm, i, 1)
+            run(load_h, i + 4)
+            run(load_rest, i + 4)
+            for t in NORM_ON_GPSIMD:
+                run(normalise, i + 1, t)
+            run(add_bias, i + 2)
             run(group_x_conv, i + 2, 0)
             run(group_x_conv, i + 2, 1)
+            run(transpose_norm, i, 0)
+            run(transpose_norm, i, 1)
+            run(transpose_words, i + 1, "xr", 0)
             run(gain_and_biases, i, 0)
-            run(gain_and_biases, i, 1)
-            run(normalise, i + 1, 0)
-            run(normalise, i + 1, 1)
-            run(add_streams, i - 1, 0)
-            run(add_streams, i - 1, 1)
-            run(group_stats, i + 5)
-            run(rstd_of_groups, i + 5)
-            run(add_bias, i + 2)
-            run(down_product, i - 2)
-            run(skip_product, i - 1, 2)
-            run(skip_product, i - 1, 3)
-            run(transpose_words, i + 2, "xr", 0)
-            run(transpose_words, i + 2, "xr", 1)
             run(transpose_norm, i, 2)
+            run(gain_and_biases, i, 1)
             run(transpose_norm, i, 3)
-            run(silu_gate, i + 2, 0)
+            run(transpose_words, i + 1, "xr", 1)
+            run(silu_gate, i + 1, 0)
             run(gain_and_biases, i, 2)
-            run(silu_gate, i + 2, 1)
             run(gain_and_biases, i, 3)
-            run(normalise, i + 1, 2)
-            run(normalise, i + 1, 3)
-            run(add_streams, i - 1, 2)
-            run(add_streams, i - 1, 3)
+            run(silu_gate, i + 1, 1)
+            for t in range(TILES):
+                if t not in NORM_ON_GPSIMD:
+                    run(normalise, i + 1, t)
             run(apply_gate, i - 1, 0)
-            run(quantise_x_conv, i + 2)
-            run(apply_gate, i - 1, 1)
             run(add_residual_and_store, i - 2)
+            run(apply_gate, i - 1, 1)
+            run(group_stats, i + 2)
+            run(rstd_of_groups, i + 2)
             run(quantise_g, i - 1)
+            run(skip_product, i, 0)
+            run(skip_product, i, 1)
+            run(skip_product, i, 2)
+            run(transpose_words, i + 3, "xc", 0)
+            run(transpose_words, i + 3, "xc", 1)
+            run(down_product, i - 1)
+            run(add_streams, i, 0)
+            run(skip_product, i, 3)
+            run(add_streams, i, 1)
+            run(quantise_x_conv, i + 2)
+            run(add_streams, i, 2)
+            run(add_streams, i, 3)
 
         with tc.manual_schedule():
-            load_h(0)
-            load_rest(0)
-            for i in range(-5, -1):
+            for i in range(-4, -1):
                 turn(i)
-            prepare_weights()
             turn(-1)
+            prepare_weights()
             prepare_vectors()
             for i in range(N_BLOCKS + 2):
                 turn(i)

@@ -21,7 +21,7 @@ TILES = 4
 BLOCK = TILES * P
 N_BLOCKS = B // BLOCK
 PAIR = 2
-NORM_ON_GPSIMD = (3,)
+NORM_ON_GPSIMD = ()
 LINE = 4
 
 FLOPS = 2 * B * PROJ * HID + 2 * B * HID * IN
@@ -329,8 +329,8 @@ def tile_mlstmblock_pc_t_kernel(
         with tc.manual_schedule():
             for i in range(-4, -1):
                 turn(i)
-            turn(-1)
             prepare_weights()
+            turn(-1)
             prepare_vectors()
             for i in range(N_BLOCKS + 2):
                 turn(i)

@@ -21,7 +21,9 @@ TILES = 4
 BLOCK = TILES * P
 N_BLOCKS = B // BLOCK
 PAIR = 2
-NORM_ON_GPSIMD = ()
+NORM_ON_VECTOR = ()
+PARTS = (slice(0, 2), slice(2, 4))
+XC_PERIOD = 4
 LINE = 4
 
 FLOPS = 2 * B * PROJ * HID + 2 * B * HID * IN
@@ -100,7 +102,8 @@ def tile_mlstmblock_pc_t_kernel(
 
         def load_h(b):
             h_blk = loads.tile([P, TILES, HID], BF16, bufs=4)
-            nc.sync.dma_start(out=h_blk[:], in_=h_blocks[b])
+            for part in PARTS if b == 0 else (slice(0, TILES),):
+                nc.sync.dma_start(out=h_blk[:, part, :], in_=h_blocks[b][:, part, :])
             tiles["h", b] = h_blk
 
         def load_rest(b):
@@ -112,29 +115,37 @@ def tile_mlstmblock_pc_t_kernel(
             nc.sync.dma_start(out=x_blk[:], in_=x_blocks[b])
             tiles["xc", b], tiles["xr", b], tiles["x", b] = xc_blk, xr_blk, x_blk
 
-        def group_stats(b):
-            stats = small.tile([P, TILES * GROUPS, 3], F32)
-            for t in range(TILES):
+        def group_stats(b, tiles_of_part):
+            if ("stats", b) not in tiles:
+                stats = small.tile([P, TILES * GROUPS, 3], F32)
+                tiles["stats", b] = stats
+            for t in range(TILES)[tiles_of_part]:
                 for two in range(GROUPS // 2):
                     nc.vector.bn_stats(
-                        out=stats[:, t * GROUPS + 2 * two : t * GROUPS + 2 * two + 2, :].rearrange("p g s -> p (g s)"),
+                        out=tiles["stats", b][:, t * GROUPS + 2 * two : t * GROUPS + 2 * two + 2, :].rearrange(
+                            "p g s -> p (g s)"
+                        ),
                         in_=tiles["h", b][:, t, 2 * two * GROUP : (2 * two + 2) * GROUP].rearrange(
                             "p (g m) -> p m g", g=2
                         ),
                     )
-            tiles["stats", b] = stats
 
-        def rstd_of_groups(b):
-            mean, m2 = tiles["stats", b][:, :, 1:2], tiles["stats", b][:, :, 2:3]
-            neg_mean = small.tile([P, TILES * GROUPS, 1], F32)
-            nc.gpsimd.tensor_scalar(out=neg_mean[:], in0=mean, scalar1=-1.0, scalar2=0.0, op0=ALU.mult, op1=ALU.add)
-            var_eps = small.tile([P, TILES * GROUPS, 1], F32)
-            nc.gpsimd.tensor_scalar(out=var_eps[:], in0=m2, scalar1=1.0 / GROUP, scalar2=EPS, op0=ALU.mult, op1=ALU.add)
-            rstd = small.tile([P, TILES * GROUPS, 1], F32)
-            nc.gpsimd.tensor_tensor(out=rstd[:], in0=var_eps[:], in1=neg_half[:], op=ALU.pow)
-            neg_mean_rstd = small.tile([P, TILES * GROUPS, 1], F32)
-            nc.gpsimd.tensor_tensor(out=neg_mean_rstd[:], in0=neg_mean[:], in1=rstd[:], op=ALU.mult)
-            tiles["rstd", b], tiles["neg_mean_rstd", b] = rstd, neg_mean_rstd
+        def rstd_of_groups(b, tiles_of_part):
+            if ("rstd", b) not in tiles:
+                neg_mean = small.tile([P, TILES * GROUPS, 1], F32)
+                var_eps = small.tile([P, TILES * GROUPS, 1], F32)
+                rstd = small.tile([P, TILES * GROUPS, 1], F32)
+                neg_mean_rstd = small.tile([P, TILES * GROUPS, 1], F32)
+                tiles["rstd", b], tiles["neg_mean_rstd", b] = rstd, neg_mean_rstd
+                tiles["neg_mean", b], tiles["var_eps", b] = neg_mean, var_eps
+            cols = slice(tiles_of_part.start * GROUPS, tiles_of_part.stop * GROUPS)
+            mean, m2 = tiles["stats", b][:, cols, 1:2], tiles["stats", b][:, cols, 2:3]
+            neg_mean, var_eps = tiles["neg_mean", b][:, cols, :], tiles["var_eps", b][:, cols, :]
+            rstd, neg_mean_rstd = tiles["rstd", b][:, cols, :], tiles["neg_mean_rstd", b][:, cols, :]
+            nc.gpsimd.tensor_scalar(out=var_eps, in0=m2, scalar1=1.0 / GROUP, scalar2=EPS, op0=ALU.mult, op1=ALU.add)
+            nc.gpsimd.tensor_tensor(out=rstd, in0=var_eps, in1=neg_half[:, cols, :], op=ALU.pow)
+            nc.gpsimd.tensor_scalar(out=neg_mean, in0=mean, scalar1=-1.0, scalar2=0.0, op0=ALU.mult, op1=ALU.add)
+            nc.gpsimd.tensor_tensor(out=neg_mean_rstd, in0=neg_mean, in1=rstd, op=ALU.mult)
 
         def add_bias(b):
             residual = held.tile([P, TILES, IN], F32, bufs=5)
@@ -146,18 +157,20 @@ def tile_mlstmblock_pc_t_kernel(
             )
             tiles["residual", b] = residual
 
-        def normalise(b, t):
+        def normalise(b, t, on_vector):
             if ("norm", b) not in tiles:
                 norm = work.tile([P, TILES, PACK, P], F32)
                 tiles["norm", b] = norm
             for j in range(GROUPS):
+                if ((t, j) in NORM_ON_VECTOR) != on_vector:
+                    continue
                 m0 = j * (P // GROUPS)
                 normed = tiles["norm", b][:, t, :, m0 : m0 + P // GROUPS]
                 raw = tiles["h", b][:, t, j * GROUP : (j + 1) * GROUP].rearrange("p (m q) -> p q m", q=PACK)
                 rstd = tiles["rstd", b][:, t * GROUPS + j, :]
                 neg_mean_rstd = tiles["neg_mean_rstd", b][:, t * GROUPS + j, :]
-                if t in NORM_ON_GPSIMD:
-                    nc.gpsimd.tensor_scalar(
+                if on_vector:
+                    nc.vector.tensor_scalar(
                         out=normed, in0=raw, scalar1=rstd, scalar2=neg_mean_rstd, op0=ALU.mult, op1=ALU.add
                     )
                 else:
@@ -175,7 +188,8 @@ def tile_mlstmblock_pc_t_kernel(
             if pair == 0:
                 xc_grouped = work.tile([P, TILES, P, PACK], BF16, align_bytes=64)
                 tiles["xc_grouped", b] = xc_grouped
-            nc.scalar.copy(
+            copy = nc.vector.tensor_copy if pair == 1 and b % XC_PERIOD == XC_PERIOD - 1 else nc.scalar.copy
+            copy(
                 out=tiles["xc_grouped", b][:].bitcast(F32)[:, pair * PAIR : (pair + 1) * PAIR, :, :],
                 in_=tiles["xc_t", b, pair][:].rearrange("p u i r -> p i r u"),
             )
@@ -242,12 +256,12 @@ def tile_mlstmblock_pc_t_kernel(
                 op=ALU.add,
             )
 
-        def apply_gate(b, pair):
-            if pair == 0:
+        def apply_gate(b, first, last, engine):
+            if ("g_grouped", b) not in tiles:
                 g_grouped = work.tile([P, BLOCK, PACK], BF16, align_bytes=64)
                 tiles["g_grouped", b] = g_grouped
-            rows = slice(pair * PAIR * P, (pair + 1) * PAIR * P)
-            nc.vector.tensor_tensor(
+            rows = slice(first * P, last * P)
+            engine.tensor_tensor(
                 out=tiles["g_grouped", b][:, rows, :],
                 in0=tiles["summed", b][:, rows, :],
                 in1=tiles["gate", b][:, rows, :],
@@ -287,49 +301,48 @@ def tile_mlstmblock_pc_t_kernel(
         def turn(i):
             run(load_h, i + 4)
             run(load_rest, i + 4)
-            for t in NORM_ON_GPSIMD:
-                run(normalise, i + 1, t)
-            run(add_bias, i + 2)
-            run(group_x_conv, i + 2, 0)
-            run(group_x_conv, i + 2, 1)
             run(transpose_norm, i, 0)
             run(transpose_norm, i, 1)
-            run(transpose_words, i + 1, "xr", 0)
+            run(silu_gate, i + 1, 0)
             run(gain_and_biases, i, 0)
             run(transpose_norm, i, 2)
             run(gain_and_biases, i, 1)
             run(transpose_norm, i, 3)
-            run(transpose_words, i + 1, "xr", 1)
-            run(silu_gate, i + 1, 0)
+            run(transpose_words, i + 2, "xc", 0)
+            run(silu_gate, i + 1, 1)
+            run(transpose_words, i + 2, "xc", 1)
             run(gain_and_biases, i, 2)
             run(gain_and_biases, i, 3)
-            run(silu_gate, i + 1, 1)
-            for t in range(TILES):
-                if t not in NORM_ON_GPSIMD:
-                    run(normalise, i + 1, t)
-            run(apply_gate, i - 1, 0)
+            run(group_x_conv, i + 2, 0)
+            run(apply_gate, i - 1, 0, 2, nc.vector)
             run(add_residual_and_store, i - 2)
-            run(apply_gate, i - 1, 1)
-            run(group_stats, i + 2)
-            run(rstd_of_groups, i + 2)
+            run(apply_gate, i - 1, 2, 4, nc.vector)
+            for part in PARTS if i + 2 == 0 else (slice(0, TILES),):
+                run(group_stats, i + 2, part)
+                if i == -1:
+                    prepare_weights()
+                run(rstd_of_groups, i + 2, part)
+            run(add_bias, i + 2)
+            run(quantise_x_conv, i + 1)
             run(quantise_g, i - 1)
+            run(group_x_conv, i + 2, 1)
+            for t in range(TILES):
+                run(normalise, i + 1, t, False)
             run(skip_product, i, 0)
             run(skip_product, i, 1)
             run(skip_product, i, 2)
-            run(transpose_words, i + 3, "xc", 0)
-            run(transpose_words, i + 3, "xc", 1)
             run(down_product, i - 1)
             run(add_streams, i, 0)
             run(skip_product, i, 3)
+            run(transpose_words, i + 2, "xr", 0)
+            run(transpose_words, i + 2, "xr", 1)
             run(add_streams, i, 1)
-            run(quantise_x_conv, i + 2)
             run(add_streams, i, 2)
             run(add_streams, i, 3)
 
         with tc.manual_schedule():
             for i in range(-4, -1):
                 turn(i)
-            prepare_weights()
             turn(-1)
             prepare_vectors()
             for i in range(N_BLOCKS + 2):

@@ -21,9 +21,8 @@ TILES = 4
 BLOCK = TILES * P
 N_BLOCKS = B // BLOCK
 PAIR = 2
-NORM_ON_VECTOR = ()
-PARTS = (slice(0, 2), slice(2, 4))
-XC_PERIOD = 4
+WHOLE = (slice(0, TILES),)
+PARTS = (slice(0, PAIR), slice(PAIR, TILES))
 LINE = 4
 
 FLOPS = 2 * B * PROJ * HID + 2 * B * HID * IN
@@ -64,9 +63,7 @@ def tile_mlstmblock_pc_t_kernel(
         for v, vec in enumerate((gn_w, gn_b, skip_b)):
             nc.scalar.dma_start(out=vec_rows[v : v + 1, :], in_=vec.unsqueeze(0))
         skip_raw = consts.tile([P, PACK, HID], BF16)
-        nc.scalar.dma_start(out=skip_raw[:], in_=skip_w.rearrange("(p k) c -> p k c", k=PACK))
         down_raw = consts.tile([P, PACK, IN], BF16)
-        nc.scalar.dma_start(out=down_raw[:], in_=down_w.rearrange("(p k) c -> p k c", k=PACK))
         down_b_all = consts.tile([P, IN], BF16)
         nc.gpsimd.dma_start(out=down_b_all[:], in_=down_b.partition_broadcast(P))
 
@@ -100,20 +97,21 @@ def tile_mlstmblock_pc_t_kernel(
 
         tiles = {}
 
-        def load_h(b):
-            h_blk = loads.tile([P, TILES, HID], BF16, bufs=4)
-            for part in PARTS if b == 0 else (slice(0, TILES),):
-                nc.sync.dma_start(out=h_blk[:, part, :], in_=h_blocks[b][:, part, :])
-            tiles["h", b] = h_blk
-
-        def load_rest(b):
+        def load(b):
             xc_blk = loads.tile([P, TILES, PROJ], BF16)
-            nc.sync.dma_start(out=xc_blk[:], in_=xc_blocks[b])
+            h_blk = loads.tile([P, TILES, HID], BF16)
             xr_blk = loads.tile([P, TILES, HID], BF16)
-            nc.sync.dma_start(out=xr_blk[:], in_=xr_blocks[b])
             x_blk = loads.tile([P, TILES, IN], BF16)
+            for part in PARTS if b == 0 else WHOLE:
+                nc.sync.dma_start(out=xc_blk[:, part, :], in_=xc_blocks[b][:, part, :])
+                nc.sync.dma_start(out=h_blk[:, part, :], in_=h_blocks[b][:, part, :])
+            for part in PARTS if b == 0 else WHOLE:
+                nc.sync.dma_start(out=xr_blk[:, part, :], in_=xr_blocks[b][:, part, :])
+                if b == 0 and part.start == 0:
+                    nc.sync.dma_start(out=skip_raw[:], in_=skip_w.rearrange("(p k) c -> p k c", k=PACK))
+                    nc.sync.dma_start(out=down_raw[:], in_=down_w.rearrange("(p k) c -> p k c", k=PACK))
             nc.sync.dma_start(out=x_blk[:], in_=x_blocks[b])
-            tiles["xc", b], tiles["xr", b], tiles["x", b] = xc_blk, xr_blk, x_blk
+            tiles["h", b], tiles["xc", b], tiles["xr", b], tiles["x", b] = h_blk, xc_blk, xr_blk, x_blk
 
         def group_stats(b, tiles_of_part):
             if ("stats", b) not in tiles:
@@ -157,19 +155,20 @@ def tile_mlstmblock_pc_t_kernel(
             )
             tiles["residual", b] = residual
 
-        def normalise(b, t, on_vector):
+        def on_vector(b, t):
+            return b == 0 and t >= PAIR
+
+        def normalise(b, t):
             if ("norm", b) not in tiles:
                 norm = work.tile([P, TILES, PACK, P], F32)
                 tiles["norm", b] = norm
             for j in range(GROUPS):
-                if ((t, j) in NORM_ON_VECTOR) != on_vector:
-                    continue
                 m0 = j * (P // GROUPS)
                 normed = tiles["norm", b][:, t, :, m0 : m0 + P // GROUPS]
                 raw = tiles["h", b][:, t, j * GROUP : (j + 1) * GROUP].rearrange("p (m q) -> p q m", q=PACK)
                 rstd = tiles["rstd", b][:, t * GROUPS + j, :]
                 neg_mean_rstd = tiles["neg_mean_rstd", b][:, t * GROUPS + j, :]
-                if on_vector:
+                if on_vector(b, t):
                     nc.vector.tensor_scalar(
                         out=normed, in0=raw, scalar1=rstd, scalar2=neg_mean_rstd, op0=ALU.mult, op1=ALU.add
                     )
@@ -188,8 +187,7 @@ def tile_mlstmblock_pc_t_kernel(
             if pair == 0:
                 xc_grouped = work.tile([P, TILES, P, PACK], BF16, align_bytes=64)
                 tiles["xc_grouped", b] = xc_grouped
-            copy = nc.vector.tensor_copy if pair == 1 and b % XC_PERIOD == XC_PERIOD - 1 else nc.scalar.copy
-            copy(
+            nc.scalar.copy(
                 out=tiles["xc_grouped", b][:].bitcast(F32)[:, pair * PAIR : (pair + 1) * PAIR, :, :],
                 in_=tiles["xc_t", b, pair][:].rearrange("p u i r -> p i r u"),
             )
@@ -268,18 +266,27 @@ def tile_mlstmblock_pc_t_kernel(
                 op=ALU.mult,
             )
 
-        def quantise_g(b):
-            g_codes = work.tile([P, TILES * P], U32, align_bytes=64)
-            g_scales = work.tile([P, TILES * P], U8, align_bytes=64)
-            quantise(nc, g_codes[:], g_scales[:], tiles["g_grouped", b][:].rearrange("p r q -> p (r q)"))
-            tiles["g_codes", b], tiles["g_scales", b] = g_codes, g_scales
+        def quantise_g(b, part):
+            if ("g_codes", b) not in tiles:
+                g_codes = work.tile([P, BLOCK], U32, align_bytes=64)
+                g_scales = work.tile([P, BLOCK], U8, align_bytes=64)
+                tiles["g_codes", b], tiles["g_scales", b] = g_codes, g_scales
+            rows = slice(part.start * P, part.stop * P)
+            quantise(
+                nc,
+                tiles["g_codes", b][:, rows],
+                tiles["g_scales", b][:, rows],
+                tiles["g_grouped", b][:, rows, :].rearrange("p r q -> p (r q)"),
+            )
 
-        def down_product(b):
-            y = psum_y.tile([P, TILES, IN], F32)
-            for t in range(TILES):
+        def down_product(b, part):
+            if ("y", b) not in tiles:
+                y = psum_y.tile([P, TILES, IN], F32)
+                tiles["y", b] = y
+            for t in range(TILES)[part]:
                 rows = slice(t * P, (t + 1) * P)
                 nc.tensor.matmul_mx(
-                    out=y[:, t, :],
+                    out=tiles["y", b][:, t, :],
                     lhsT=tiles["g_codes", b][:, rows].bitcast(FP8X4),
                     lhsT_scale=tiles["g_scales", b][:, rows],
                     rhs=down_codes[:].bitcast(FP8X4),
@@ -287,20 +294,23 @@ def tile_mlstmblock_pc_t_kernel(
                     start=True,
                     stop=True,
                 )
-            tiles["y", b] = y
 
-        def add_residual_and_store(b):
-            result = work.tile([P, TILES, IN], F32)
-            nc.vector.tensor_tensor(out=result[:], in0=tiles["y", b][:], in1=tiles["residual", b][:], op=ALU.add)
-            nc.sync.dma_start(out=out_blocks[b], in_=result[:])
+        def add_residual_and_store(b, part):
+            if ("result", b) not in tiles:
+                result = work.tile([P, TILES, IN], F32)
+                tiles["result", b] = result
+            result = tiles["result", b][:, part, :]
+            nc.vector.tensor_tensor(
+                out=result, in0=tiles["y", b][:, part, :], in1=tiles["residual", b][:, part, :], op=ALU.add
+            )
+            nc.sync.dma_start(out=out_blocks[b][:, part, :], in_=result)
 
         def run(piece, b, *part):
             if 0 <= b < N_BLOCKS:
                 piece(b, *part)
 
         def turn(i):
-            run(load_h, i + 4)
-            run(load_rest, i + 4)
+            run(load, i + 4)
             run(transpose_norm, i, 0)
             run(transpose_norm, i, 1)
             run(silu_gate, i + 1, 0)
@@ -314,24 +324,32 @@ def tile_mlstmblock_pc_t_kernel(
             run(gain_and_biases, i, 2)
             run(gain_and_biases, i, 3)
             run(group_x_conv, i + 2, 0)
-            run(apply_gate, i - 1, 0, 2, nc.vector)
-            run(add_residual_and_store, i - 2)
-            run(apply_gate, i - 1, 2, 4, nc.vector)
-            for part in PARTS if i + 2 == 0 else (slice(0, TILES),):
-                run(group_stats, i + 2, part)
-                if i == -1:
-                    prepare_weights()
-                run(rstd_of_groups, i + 2, part)
-            run(add_bias, i + 2)
-            run(quantise_x_conv, i + 1)
-            run(quantise_g, i - 1)
             run(group_x_conv, i + 2, 1)
+            run(apply_gate, i - 1, 0, 2, nc.vector)
+            for part in PARTS if i - 2 == N_BLOCKS - 1 else WHOLE:
+                run(add_residual_and_store, i - 2, part)
+            run(apply_gate, i - 1, 2, 4, nc.vector)
+            for part in PARTS if i + 2 == 0 else WHOLE:
+                run(group_stats, i + 2, part)
+                run(rstd_of_groups, i + 2, part)
+            if i == -2:
+                prepare_weights()
+                prepare_vectors()
+            run(add_bias, i + 2)
             for t in range(TILES):
-                run(normalise, i + 1, t, False)
+                if on_vector(i + 1, t):
+                    run(normalise, i + 1, t)
+            run(quantise_x_conv, i + 1)
+            for part in PARTS if i - 1 == N_BLOCKS - 1 else WHOLE:
+                run(quantise_g, i - 1, part)
+            for t in range(TILES):
+                if not on_vector(i + 1, t):
+                    run(normalise, i + 1, t)
             run(skip_product, i, 0)
             run(skip_product, i, 1)
             run(skip_product, i, 2)
-            run(down_product, i - 1)
+            for part in PARTS if i - 1 == N_BLOCKS - 1 else WHOLE:
+                run(down_product, i - 1, part)
             run(add_streams, i, 0)
             run(skip_product, i, 3)
             run(transpose_words, i + 2, "xr", 0)
@@ -341,9 +359,5 @@ def tile_mlstmblock_pc_t_kernel(
             run(add_streams, i, 3)
 
         with tc.manual_schedule():
-            for i in range(-4, -1):
-                turn(i)
-            turn(-1)
-            prepare_vectors()
-            for i in range(N_BLOCKS + 2):
+            for i in range(-4, N_BLOCKS + 2):
                 turn(i)

from contextlib import ExitStack

import concourse.mybir as mybir
from concourse.masks import make_identity

F32 = mybir.dt.float32
BF16 = mybir.dt.bfloat16
U32 = mybir.dt.uint32
U8 = mybir.dt.uint8
FP8X4 = mybir.dt.float8_e4m3fn_x4
ALU = mybir.AluOpType
ACT = mybir.ActivationFunctionType

P = 128
PACK = 4
B, IN, HID, PROJ = 8192, 128, 512, 512
GROUPS = 4
GROUP = HID // GROUPS
EPS = 1e-5
TILES = 4
BLOCK = TILES * P
N_BLOCKS = B // BLOCK
PAIR = 2
WHOLE = (slice(0, TILES),)
PARTS = (slice(0, PAIR), slice(PAIR, TILES))
LINE = 4

FLOPS = 2 * B * PROJ * HID + 2 * B * HID * IN


def quantise(nc, codes, scales, grouped):
    nc.vector.quantize_mx(out=codes.bitcast(FP8X4), scales=scales, in_=grouped)


def tile_mlstmblock_pc_t_kernel(
    tc, h_t, x_conv, x_right, x, gn_w, gn_b, skip_w, skip_b, down_w, down_b, out
):
    nc = tc.nc
    h_blocks = h_t.rearrange("(b p t) c -> b p t c", p=P, t=TILES)
    xc_blocks = x_conv.rearrange("(b p t) c -> b p t c", p=P, t=TILES)
    xr_blocks = x_right.rearrange("(b p t) c -> b p t c", p=P, t=TILES)
    x_blocks = x.rearrange("(b p t) c -> b p t c", p=P, t=TILES)
    out_blocks = out.rearrange("(b p t) c -> b p t c", p=P, t=TILES)

    with ExitStack() as ctx:
        consts = ctx.enter_context(tc.tile_pool(name="consts", bufs=1))
        loads = ctx.enter_context(tc.tile_pool(name="loads", bufs=4))
        work = ctx.enter_context(tc.tile_pool(name="work", bufs=2))
        held = ctx.enter_context(tc.tile_pool(name="held", bufs=4))
        small = ctx.enter_context(tc.tile_pool(name="small", bufs=6))
        psum_in = ctx.enter_context(tc.psum_pool(name="psum_in", bufs=2))
        psum_norm = ctx.enter_context(tc.psum_pool(name="psum_norm", bufs=2))
        psum_skip = ctx.enter_context(tc.psum_pool(name="psum_skip", bufs=3))
        psum_y = ctx.enter_context(tc.psum_pool(name="psum_y", bufs=1))

        ident_f32 = consts.tile([P, P], F32)
        make_identity(nc, ident_f32[:])
        neg_half = consts.tile([P, TILES * GROUPS, 1], F32)
        nc.vector.memset(neg_half[:], -0.5)

        vec_rows = consts.tile([P, HID], BF16)
        nc.vector.memset(vec_rows[:], 0.0)
        for v, vec in enumerate((gn_w, gn_b, skip_b)):
            nc.scalar.dma_start(out=vec_rows[v : v + 1, :], in_=vec.unsqueeze(0))
        skip_raw = consts.tile([P, PACK, HID], BF16)
        down_raw = consts.tile([P, PACK, IN], BF16)
        down_b_all = consts.tile([P, IN], BF16)
        nc.gpsimd.dma_start(out=down_b_all[:], in_=down_b.partition_broadcast(P))

        skip_codes = consts.tile([P, HID], U32, align_bytes=64)
        skip_scales = consts.tile([P, HID], U8, align_bytes=64)
        down_codes = consts.tile([P, IN], U32, align_bytes=64)
        down_scales = consts.tile([P, IN], U8, align_bytes=64)
        vec_cols = consts.tile([P, 3 * PACK], F32)
        gain = vec_cols[:, 0:PACK]
        shift = consts.tile([P, PACK], F32)

        def prepare_weights():
            skip_grouped = consts.tile([P, PACK, P, PACK], BF16, align_bytes=64)
            nc.vector.tensor_copy(out=skip_grouped[:], in_=skip_raw[:].rearrange("p k (m q) -> p q m k", q=PACK))
            down_grouped = consts.tile([P, IN, PACK], BF16, align_bytes=64)
            nc.vector.tensor_copy(out=down_grouped[:], in_=down_raw[:].rearrange("p k c -> p c k"))
            quantise(nc, skip_codes[:], skip_scales[:], skip_grouped[:].rearrange("p q m k -> p (q m k)"))
            quantise(nc, down_codes[:], down_scales[:], down_grouped[:].rearrange("p c k -> p (c k)"))

        def prepare_vectors():
            vec_t = psum_y.tile([P, TILES, IN], F32, tag="y")
            for u in range(2):
                nc.tensor.transpose(vec_t[:, u, :], vec_rows[:].bitcast(F32)[:, u::2], ident_f32[:])
            nc.vector.tensor_copy(
                out=vec_cols[:].rearrange("p (v u e) -> p v u e", v=3, u=2),
                in_=vec_t[:, 0:2, :].bitcast(BF16)[:, :, 0:6].rearrange("p u (v e) -> p v u e", v=3),
            )
            nc.vector.tensor_tensor(
                out=shift[:], in0=vec_cols[:, PACK : 2 * PACK], in1=vec_cols[:, 2 * PACK : 3 * PACK], op=ALU.add
            )

        tiles = {}

        def load(b):
            xc_blk = loads.tile([P, TILES, PROJ], BF16)
            h_blk = loads.tile([P, TILES, HID], BF16)
            xr_blk = loads.tile([P, TILES, HID], BF16)
            x_blk = loads.tile([P, TILES, IN], BF16)
            for part in PARTS if b == 0 else WHOLE:
                nc.sync.dma_start(out=xc_blk[:, part, :], in_=xc_blocks[b][:, part, :])
                nc.sync.dma_start(out=h_blk[:, part, :], in_=h_blocks[b][:, part, :])
            for part in PARTS if b == 0 else WHOLE:
                nc.sync.dma_start(out=xr_blk[:, part, :], in_=xr_blocks[b][:, part, :])
                if b == 0 and part.start == 0:
                    nc.sync.dma_start(out=skip_raw[:], in_=skip_w.rearrange("(p k) c -> p k c", k=PACK))
                    nc.sync.dma_start(out=down_raw[:], in_=down_w.rearrange("(p k) c -> p k c", k=PACK))
            nc.sync.dma_start(out=x_blk[:], in_=x_blocks[b])
            tiles["h", b], tiles["xc", b], tiles["xr", b], tiles["x", b] = h_blk, xc_blk, xr_blk, x_blk

        def group_stats(b, tiles_of_part):
            if ("stats", b) not in tiles:
                stats = small.tile([P, TILES * GROUPS, 3], F32)
                tiles["stats", b] = stats
            for t in range(TILES)[tiles_of_part]:
                for two in range(GROUPS // 2):
                    nc.vector.bn_stats(
                        out=tiles["stats", b][:, t * GROUPS + 2 * two : t * GROUPS + 2 * two + 2, :].rearrange(
                            "p g s -> p (g s)"
                        ),
                        in_=tiles["h", b][:, t, 2 * two * GROUP : (2 * two + 2) * GROUP].rearrange(
                            "p (g m) -> p m g", g=2
                        ),
                    )

        def rstd_of_groups(b, tiles_of_part):
            if ("rstd", b) not in tiles:
                neg_mean = small.tile([P, TILES * GROUPS, 1], F32)
                var_eps = small.tile([P, TILES * GROUPS, 1], F32)
                rstd = small.tile([P, TILES * GROUPS, 1], F32)
                neg_mean_rstd = small.tile([P, TILES * GROUPS, 1], F32)
                tiles["rstd", b], tiles["neg_mean_rstd", b] = rstd, neg_mean_rstd
                tiles["neg_mean", b], tiles["var_eps", b] = neg_mean, var_eps
            cols = slice(tiles_of_part.start * GROUPS, tiles_of_part.stop * GROUPS)
            mean, m2 = tiles["stats", b][:, cols, 1:2], tiles["stats", b][:, cols, 2:3]
            neg_mean, var_eps = tiles["neg_mean", b][:, cols, :], tiles["var_eps", b][:, cols, :]
            rstd, neg_mean_rstd = tiles["rstd", b][:, cols, :], tiles["neg_mean_rstd", b][:, cols, :]
            nc.gpsimd.tensor_scalar(out=var_eps, in0=m2, scalar1=1.0 / GROUP, scalar2=EPS, op0=ALU.mult, op1=ALU.add)
            nc.gpsimd.tensor_tensor(out=rstd, in0=var_eps, in1=neg_half[:, cols, :], op=ALU.pow)
            nc.gpsimd.tensor_scalar(out=neg_mean, in0=mean, scalar1=-1.0, scalar2=0.0, op0=ALU.mult, op1=ALU.add)
            nc.gpsimd.tensor_tensor(out=neg_mean_rstd, in0=neg_mean, in1=rstd, op=ALU.mult)

        def add_bias(b):
            residual = held.tile([P, TILES, IN], F32, bufs=5)
            nc.gpsimd.tensor_tensor(
                out=residual[:],
                in0=tiles["x", b][:],
                in1=down_b_all[:].unsqueeze(1).to_broadcast([P, TILES, IN]),
                op=ALU.add,
            )
            tiles["residual", b] = residual

        def on_vector(b, t):
            return b == 0 and t >= PAIR

        def normalise(b, t):
            if ("norm", b) not in tiles:
                norm = work.tile([P, TILES, PACK, P], F32)
                tiles["norm", b] = norm
            for j in range(GROUPS):
                m0 = j * (P // GROUPS)
                normed = tiles["norm", b][:, t, :, m0 : m0 + P // GROUPS]
                raw = tiles["h", b][:, t, j * GROUP : (j + 1) * GROUP].rearrange("p (m q) -> p q m", q=PACK)
                rstd = tiles["rstd", b][:, t * GROUPS + j, :]
                neg_mean_rstd = tiles["neg_mean_rstd", b][:, t * GROUPS + j, :]
                if on_vector(b, t):
                    nc.vector.tensor_scalar(
                        out=normed, in0=raw, scalar1=rstd, scalar2=neg_mean_rstd, op0=ALU.mult, op1=ALU.add
                    )
                else:
                    nc.scalar.activation(out=normed, in_=raw, func=ACT.Identity, scale=rstd, bias=neg_mean_rstd)

        def transpose_words(b, name, pair):
            words = tiles[name, b][:].bitcast(F32)
            in_t = psum_in.tile([P, 2, PAIR, P], F32)
            for i in range(PAIR):
                for u in range(2):
                    nc.tensor.transpose(in_t[:, u, i, :], words[:, pair * PAIR + i, u::2], ident_f32[:])
            tiles[name + "_t", b, pair] = in_t

        def group_x_conv(b, pair):
            if pair == 0:
                xc_grouped = work.tile([P, TILES, P, PACK], BF16, align_bytes=64)
                tiles["xc_grouped", b] = xc_grouped
            nc.scalar.copy(
                out=tiles["xc_grouped", b][:].bitcast(F32)[:, pair * PAIR : (pair + 1) * PAIR, :, :],
                in_=tiles["xc_t", b, pair][:].rearrange("p u i r -> p i r u"),
            )

        def quantise_x_conv(b):
            xc_codes = held.tile([P, TILES * P], U32, align_bytes=64)
            xc_scales = held.tile([P, TILES * P], U8, align_bytes=64)
            quantise(nc, xc_codes[:], xc_scales[:], tiles["xc_grouped", b][:].rearrange("p t r q -> p (t r q)"))
            tiles["xc_codes", b], tiles["xc_scales", b] = xc_codes, xc_scales

        def silu_gate(b, pair):
            if pair == 0:
                gate = held.tile([P, BLOCK, PACK], F32)
                tiles["gate", b] = gate
            rows = slice(pair * PAIR * P, (pair + 1) * PAIR * P)
            nc.scalar.activation(
                out=tiles["gate", b][:, rows, :].rearrange("p r (u e) -> p r u e", e=2),
                in_=tiles["xr_t", b, pair][:].rearrange("p u i r -> p u (i r)").bitcast(BF16).rearrange("p u (r e) -> p r u e", e=2),
                func=ACT.Silu,
            )

        def transpose_norm(b, q):
            norm_t = psum_norm.tile([P, TILES, P], F32)
            for t in range(TILES):
                nc.tensor.transpose(norm_t[:, t, :], tiles["norm", b][:, t, q, :], ident_f32[:])
            tiles["norm_t", b, q] = norm_t

        def gain_and_biases(b, q):
            if q == 0:
                gn = work.tile([P, PACK, TILES, P], F32)
                tiles["gn", b] = gn
            nc.scalar.activation(
                out=tiles["gn", b][:, q, :, :],
                in_=tiles["norm_t", b, q][:],
                func=ACT.Identity,
                scale=gain[:, q : q + 1],
                bias=shift[:, q : q + 1],
            )

        def skip_product(b, t):
            rows = slice(t * P, (t + 1) * P)
            skip_t = psum_skip.tile([P, PACK, P], F32)
            for q in range(PACK):
                cols = slice(q * P, (q + 1) * P)
                nc.tensor.matmul_mx(
                    out=skip_t[:, q, :],
                    lhsT=skip_codes[:, cols].bitcast(FP8X4),
                    lhsT_scale=skip_scales[:, cols],
                    rhs=tiles["xc_codes", b][:, rows].bitcast(FP8X4),
                    rhs_scale=tiles["xc_scales", b][:, rows],
                    start=True,
                    stop=True,
                )
            tiles["skip_t", b, t] = skip_t

        def add_streams(b, t):
            if t == 0:
                summed = work.tile([P, BLOCK, PACK], F32)
                tiles["summed", b] = summed
            nc.vector.tensor_tensor(
                out=tiles["summed", b][:, t * P : (t + 1) * P, :].rearrange("p (c i) q -> p c q i", i=LINE),
                in0=tiles["skip_t", b, t][:].rearrange("p q (c i) -> p c q i", i=LINE),
                in1=tiles["gn", b][:, :, t, :].rearrange("p q (c i) -> p c q i", i=LINE),
                op=ALU.add,
            )

        def apply_gate(b, first, last, engine):
            if ("g_grouped", b) not in tiles:
                g_grouped = work.tile([P, BLOCK, PACK], BF16, align_bytes=64)
                tiles["g_grouped", b] = g_grouped
            rows = slice(first * P, last * P)
            engine.tensor_tensor(
                out=tiles["g_grouped", b][:, rows, :],
                in0=tiles["summed", b][:, rows, :],
                in1=tiles["gate", b][:, rows, :],
                op=ALU.mult,
            )

        def quantise_g(b, part):
            if ("g_codes", b) not in tiles:
                g_codes = work.tile([P, BLOCK], U32, align_bytes=64)
                g_scales = work.tile([P, BLOCK], U8, align_bytes=64)
                tiles["g_codes", b], tiles["g_scales", b] = g_codes, g_scales
            rows = slice(part.start * P, part.stop * P)
            quantise(
                nc,
                tiles["g_codes", b][:, rows],
                tiles["g_scales", b][:, rows],
                tiles["g_grouped", b][:, rows, :].rearrange("p r q -> p (r q)"),
            )

        def down_product(b, part):
            if ("y", b) not in tiles:
                y = psum_y.tile([P, TILES, IN], F32)
                tiles["y", b] = y
            for t in range(TILES)[part]:
                rows = slice(t * P, (t + 1) * P)
                nc.tensor.matmul_mx(
                    out=tiles["y", b][:, t, :],
                    lhsT=tiles["g_codes", b][:, rows].bitcast(FP8X4),
                    lhsT_scale=tiles["g_scales", b][:, rows],
                    rhs=down_codes[:].bitcast(FP8X4),
                    rhs_scale=down_scales[:],
                    start=True,
                    stop=True,
                )

        def add_residual_and_store(b, part):
            if ("result", b) not in tiles:
                result = work.tile([P, TILES, IN], F32)
                tiles["result", b] = result
            result = tiles["result", b][:, part, :]
            nc.vector.tensor_tensor(
                out=result, in0=tiles["y", b][:, part, :], in1=tiles["residual", b][:, part, :], op=ALU.add
            )
            nc.sync.dma_start(out=out_blocks[b][:, part, :], in_=result)

        def run(piece, b, *part):
            if 0 <= b < N_BLOCKS:
                piece(b, *part)

        def turn(i):
            run(load, i + 4)
            run(transpose_norm, i, 0)
            run(transpose_norm, i, 1)
            run(silu_gate, i + 1, 0)
            run(gain_and_biases, i, 0)
            run(transpose_norm, i, 2)
            run(gain_and_biases, i, 1)
            run(transpose_norm, i, 3)
            run(transpose_words, i + 2, "xc", 0)
            run(silu_gate, i + 1, 1)
            run(transpose_words, i + 2, "xc", 1)
            run(gain_and_biases, i, 2)
            run(gain_and_biases, i, 3)
            run(group_x_conv, i + 2, 0)
            run(group_x_conv, i + 2, 1)
            run(apply_gate, i - 1, 0, 2, nc.vector)
            for part in PARTS if i - 2 == N_BLOCKS - 1 else WHOLE:
                run(add_residual_and_store, i - 2, part)
            run(apply_gate, i - 1, 2, 4, nc.vector)
            for part in PARTS if i + 2 == 0 else WHOLE:
                run(group_stats, i + 2, part)
                run(rstd_of_groups, i + 2, part)
            if i == -2:
                prepare_weights()
                prepare_vectors()
            run(add_bias, i + 2)
            for t in range(TILES):
                if on_vector(i + 1, t):
                    run(normalise, i + 1, t)
            run(quantise_x_conv, i + 1)
            for part in PARTS if i - 1 == N_BLOCKS - 1 else WHOLE:
                run(quantise_g, i - 1, part)
            for t in range(TILES):
                if not on_vector(i + 1, t):
                    run(normalise, i + 1, t)
            run(skip_product, i, 0)
            run(skip_product, i, 1)
            run(skip_product, i, 2)
            for part in PARTS if i - 1 == N_BLOCKS - 1 else WHOLE:
                run(down_product, i - 1, part)
            run(add_streams, i, 0)
            run(skip_product, i, 3)
            run(transpose_words, i + 2, "xr", 0)
            run(transpose_words, i + 2, "xr", 1)
            run(add_streams, i, 1)
            run(add_streams, i, 2)
            run(add_streams, i, 3)

        with tc.manual_schedule():
            for i in range(-4, N_BLOCKS + 2):
                turn(i)
